import numpy as np
import ml_dtypes


def mxq(x, axis, fmt="e4m3"):
    dtype, down = {"e4m3": (ml_dtypes.float8_e4m3fn, 7), "e5m2": (ml_dtypes.float8_e5m2, 14)}[fmt]
    v = np.moveaxis(np.asarray(x, np.float32).astype(ml_dtypes.bfloat16).astype(np.float64), axis, -1)
    blocks = v.reshape(v.shape[:-1] + (-1, 32))
    amax = np.abs(blocks).max(-1, keepdims=True)
    byte = np.maximum(np.where(amax > 0, np.frexp(amax)[1] - 1 + 127, 0) - down, 1)
    scale = np.exp2(byte - 127.0)
    codes = (blocks / scale).astype(np.float32).astype(dtype).astype(np.float64)
    return np.moveaxis((codes * scale).reshape(v.shape), -1, axis)


WIDE = False


def mx_kscale(k):
    if not WIDE:
        return np.ones(k)
    levels = np.array([10, -10, 5, -5, 0])
    a = np.random.permutation(np.resize(levels, k // 512 * 4)).reshape(k // 512, 4)
    idx = np.arange(k)
    return np.exp2(a[idx // 512, idx % 128 // 32])


BF16 = ml_dtypes.bfloat16


def bf(x):
    return np.asarray(x, np.float32).astype(BF16)


def f64(x):
    return np.asarray(x).astype(np.float64)


N, K, IN, HID, OUT = 128, 4, 512, 512, 512
NEG_SLOPE = 0.01


def leaky_relu(v):
    return np.where(v >= 0, v, NEG_SLOPE * v)


def safediv(a, b):
    return a / np.where(b == 0, np.ones_like(b), b)


def setup_inputs():
    s = mx_kscale(IN)
    u = mx_kscale(IN + HID)
    un, t = u[:IN], u[IN:]
    g = np.concatenate([np.full(IN, 1.0), np.full(HID, 3.0)])
    centre = np.random.standard_normal((N, 1, IN))
    return {"h_node": bf(np.random.standard_normal((N, IN)) * un),
            "h_ngbrs": bf((0.7 * centre + 0.7 * np.random.standard_normal((N, K, IN))) * s),
            "alpha": bf(np.random.uniform(0.0, 1.0, (N, K, 1))),
            "Wq": bf(np.random.standard_normal((HID, IN)) / np.sqrt(IN) * t[:, None] / s[None, :]),
            "bq": bf((-0.5 + 0.3 * np.random.standard_normal(HID)) * t),
            "Ww": bf(np.random.standard_normal((OUT, IN + HID)) * g[None, :] / np.sqrt(IN + HID) / u[None, :]),
            "bw": bf(-0.8 + 0.3 * np.random.standard_normal(OUT))}


def reference(h_node, h_ngbrs, alpha, Wq, bq, Ww, bw):
    a = f64(alpha)
    h1 = leaky_relu((mxq(f64(h_ngbrs), 2, "e4m3") @ mxq(f64(Wq), 1, "e4m3").T) + f64(bq))
    h_agg = safediv((a * h1).sum(axis=1), a.sum(axis=1))
    h_concat = np.concatenate([f64(h_node), h_agg], axis=-1)
    h2 = leaky_relu((mxq(h_concat, 1, "e4m3") @ mxq(f64(Ww), 1, "e4m3").T) + f64(bw))
    nrm = np.sqrt((h2 ** 2).sum(axis=-1, keepdims=True))
    return safediv(h2, nrm)

@@ -1,0 +1,240 @@
+from contextlib import ExitStack
+
+import concourse.mybir as mybir
+from concourse.masks import make_identity
+
+F32 = mybir.dt.float32
+BF16 = mybir.dt.bfloat16
+U32 = mybir.dt.uint32
+U8 = mybir.dt.uint8
+FP8X4 = mybir.dt.float8_e4m3fn_x4
+ALU = mybir.AluOpType
+ACT = mybir.ActivationFunctionType
+AXIS = mybir.AxisListType
+
+P = 128
+NGBR = 4
+PACK = 4
+K_PASS = P * PACK
+WORDS = K_PASS // 2
+IN, HID, OUT = 512, 512, 512
+NEG_SLOPE = 0.01
+
+FLOPS = 2 * (P * NGBR) * IN * HID + 2 * P * (IN + HID) * OUT
+
+
+def turn_blocks(nc, banks, ident, blocks, grouped, copy):
+    rows = P * len(blocks)
+    bank = banks.tile([P, 2, rows], F32, tag="bank")
+    for b, block in enumerate(blocks):
+        for u in range(2):
+            nc.tensor.transpose(bank[:, u, b * P : (b + 1) * P], block[:, u * P : (u + 1) * P], ident)
+    copy(out=grouped.rearrange("p (r u) -> p r u", u=2), in_=bank[:].rearrange("p u r -> p r u"))
+
+
+def quantise(nc, grouped, codes, scales):
+    nc.vector.quantize_mx(out=codes.bitcast(FP8X4), scales=scales, in_=grouped)
+
+
+def leaky_relu(nc, out, in_):
+    nc.vector.scalar_tensor_tensor(out=out, in0=in_, scalar=NEG_SLOPE, in1=in_, op0=ALU.mult, op1=ALU.max)
+
+
+def one_where_zero(nc, out, in_):
+    nc.vector.scalar_tensor_tensor(out=out, in0=in_, scalar=0.0, in1=in_, op0=ALU.is_equal, op1=ALU.add)
+
+
+def tile_pinsageconv_s_kernel(tc, h_node, h_ngbrs, alpha, Wq, bq, Ww, bw, out):
+    nc = tc.nc
+    with ExitStack() as ctx:
+        keep = ctx.enter_context(tc.tile_pool(name="keep", bufs=1))
+        work = ctx.enter_context(tc.tile_pool(name="work", bufs=4))
+        held = ctx.enter_context(tc.psum_pool(name="held", bufs=1))
+        banks = ctx.enter_context(tc.psum_pool(name="banks", bufs=6))
+
+        alpha_sb = keep.tile([P, NGBR], BF16)
+        nc.scalar.dma_start(out=alpha_sb[:], in_=alpha.rearrange("n k o -> n (k o)"))
+        bq_bf = keep.tile([P, PACK], BF16)
+        nc.scalar.dma_start(
+            out=bq_bf[:].rearrange("p (u e) -> p u e", e=2), in_=bq.rearrange("(u p e) -> p u e", u=2, e=2)
+        )
+
+        x_rows = keep.tile([P, NGBR * IN], BF16)
+        x_dram = h_ngbrs.rearrange("n k i -> n (k i)")
+        wq_rows = keep.tile([P, PACK * IN], BF16)
+        ww_rows = keep.tile([P, 4 * (IN + HID)], BF16)
+        hn_rows = keep.tile([P, IN], BF16)
+        bw_all = keep.tile([P, OUT], BF16)
+        half = 2 * IN
+        for h in range(2):
+            nc.sync.dma_start(out=x_rows[:, h * half : (h + 1) * half], in_=x_dram[:, h * half : (h + 1) * half])
+        for u in range(2):
+            nc.sync.dma_start(
+                out=wq_rows[:, u * half : (u + 1) * half],
+                in_=Wq[u * 2 * P : (u + 1) * 2 * P, :].rearrange("(p e) i -> p (e i)", e=2),
+            )
+        for h in range(2):
+            nc.sync.dma_start(
+                out=ww_rows[:, h * 2 * (IN + HID) : (h + 1) * 2 * (IN + HID)].rearrange("p (r j) -> p r j", r=2),
+                in_=Ww[h * 2 * P : (h + 1) * 2 * P, :].rearrange("(r p) j -> p r j", p=P),
+            )
+        nc.sync.dma_start(out=hn_rows[:], in_=h_node)
+        nc.sync.dma_start(out=bw_all[:], in_=bw.partition_broadcast(P))
+
+        ident = keep.tile([P, P], F32)
+        make_identity(nc, ident[:])
+        one = keep.tile([P, 1], F32)
+        nc.vector.memset(one[:], 1.0)
+        root_of_one = keep.tile([P, 1], F32)
+        nc.scalar.activation(out=root_of_one[:], in_=one[:], func=ACT.Sqrt)
+
+        alpha_sum = keep.tile([P, 1], F32)
+        nc.vector.tensor_reduce(out=alpha_sum[:], in_=alpha_sb[:], axis=AXIS.X, op=ALU.add)
+        alpha_den = keep.tile([P, 1], F32)
+        one_where_zero(nc, alpha_den[:], alpha_sum[:])
+        alpha_rec = keep.tile([P, 1], F32)
+        nc.vector.reciprocal(out=alpha_rec[:], in_=alpha_den[:])
+        w_rep = keep.tile([P, NGBR, P], F32)
+        nc.vector.tensor_scalar(
+            out=w_rep[:],
+            in0=alpha_sb[:].unsqueeze(2).to_broadcast([P, NGBR, P]),
+            scalar1=alpha_rec[:, 0:1],
+            scalar2=None,
+            op0=ALU.mult,
+        )
+        bq_col = keep.tile([P, PACK], F32)
+        nc.vector.tensor_copy(out=bq_col[:], in_=bq_bf[:])
+
+        x_words = x_rows[:].bitcast(F32)
+        wq_words = wq_rows[:].bitcast(F32)
+        x_grp = keep.tile([P, PACK * NGBR * P], BF16, align_bytes=64)
+        wq_grp = keep.tile([P, PACK * HID], BF16, align_bytes=64)
+        x_codes = keep.tile([P, NGBR * P], U32, align_bytes=64)
+        x_scales = keep.tile([P, NGBR * P], U8, align_bytes=64)
+        wq_codes = keep.tile([P, HID], U32, align_bytes=64)
+        wq_scales = keep.tile([P, HID], U8, align_bytes=64)
+        copies = [nc.scalar.copy, nc.vector.tensor_copy]
+        for words, grp in ((x_words, x_grp), (wq_words, wq_grp)):
+            grp_words = grp[:].bitcast(F32)
+            for h in range(2):
+                turn_blocks(
+                    nc,
+                    banks,
+                    ident[:],
+                    [words[:, b * WORDS : (b + 1) * WORDS] for b in (2 * h, 2 * h + 1)],
+                    grp_words[:, h * 4 * P : (h + 1) * 4 * P],
+                    copies[h],
+                )
+        w_all = held.tile([P, NGBR, P], F32)
+        for k in range(NGBR):
+            nc.tensor.transpose(w_all[:, k, :], w_rep[:, k, :], ident[:])
+        quantise(nc, x_grp[:], x_codes[:], x_scales[:])
+        quantise(nc, wq_grp[:], wq_codes[:], wq_scales[:])
+
+        h1_acc = []
+        for t in range(PACK):
+            acc = banks.tile([P, NGBR * P], F32, tag="bank", name="h1_acc%d" % t)
+            nc.tensor.matmul_mx(
+                out=acc[:],
+                lhsT=wq_codes[:, t * P : (t + 1) * P].bitcast(FP8X4),
+                lhsT_scale=wq_scales[:, t * P : (t + 1) * P],
+                rhs=x_codes[:].bitcast(FP8X4),
+                rhs_scale=x_scales[:],
+                start=True,
+                stop=True,
+            )
+            h1_acc.append(acc)
+        pre = []
+        for t in range(PACK):
+            pre_t = work.tile([P, NGBR * P], F32, name="pre%d" % t, tag="pre")
+            nc.scalar.activation(
+                out=pre_t[:], in_=h1_acc[t][:], func=ACT.Identity, bias=bq_col[:, t : t + 1], scale=1.0
+            )
+            pre.append(pre_t)
+
+        ww_words = ww_rows[:].bitcast(F32)
+        ww_grp = keep.tile([P, 2 * PACK * OUT], BF16, align_bytes=64)
+        ww_grp_words = ww_grp[:].bitcast(F32)
+        ww_codes = keep.tile([P, 2 * OUT], U32, align_bytes=64)
+        ww_scales = keep.tile([P, 2 * OUT], U8, align_bytes=64)
+        hn_grp = keep.tile([P, PACK * P], BF16, align_bytes=64)
+        hn_codes = keep.tile([P, P], U32, align_bytes=64)
+        hn_scales = keep.tile([P, P], U8, align_bytes=64)
+        for g in range(2):
+            for h in range(2):
+                turn_blocks(
+                    nc,
+                    banks,
+                    ident[:],
+                    [ww_words[:, (2 * r + g) * WORDS : (2 * r + g + 1) * WORDS] for r in (2 * h, 2 * h + 1)],
+                    ww_grp_words[:, (2 * g + h) * 4 * P : (2 * g + h + 1) * 4 * P],
+                    nc.scalar.copy,
+                )
+        turn_blocks(nc, banks, ident[:], [hn_rows[:].bitcast(F32)], hn_grp[:].bitcast(F32), nc.scalar.copy)
+
+        h2_acc = held.tile([P, OUT], F32)
+
+        def second_matmul_pass(g, codes, scales):
+            nc.tensor.matmul_mx(
+                out=h2_acc[:],
+                lhsT=codes[:].bitcast(FP8X4),
+                lhsT_scale=scales[:],
+                rhs=ww_codes[:, g * OUT : (g + 1) * OUT].bitcast(FP8X4),
+                rhs_scale=ww_scales[:, g * OUT : (g + 1) * OUT],
+                start=(g == 0),
+                stop=(g == 1),
+            )
+
+        ha_grp = keep.tile([P, P, PACK], BF16, align_bytes=64)
+        for pair in range(2):
+            blocks = (2 * pair, 2 * pair + 1)
+            h1 = {}
+            weighted = {}
+            for t in blocks:
+                h1[t] = work.tile([P, NGBR * P], F32, name="h1_%d" % t, tag="h1")
+                leaky_relu(nc, h1[t][:], pre[t][:])
+            for t in blocks:
+                weighted[t] = work.tile([P, NGBR * P], F32, name="weighted%d" % t, tag="weighted")
+                nc.vector.tensor_tensor(
+                    out=weighted[t][:], in0=h1[t][:], in1=w_all[:].rearrange("p k n -> p (k n)"), op=ALU.mult
+                )
+            for t in blocks:
+                with nc.allow_low_precision(reason="the sum is float32; h_agg is rounded once to bfloat16"):
+                    nc.vector.tensor_reduce(
+                        out=ha_grp[:, :, t],
+                        in_=weighted[t][:].rearrange("p (k n) -> p n k", k=NGBR),
+                        axis=AXIS.X,
+                        op=ALU.add,
+                    )
+            if pair == 0:
+                for g in range(2):
+                    quantise(
+                        nc,
+                        ww_grp[:, g * PACK * OUT : (g + 1) * PACK * OUT],
+                        ww_codes[:, g * OUT : (g + 1) * OUT],
+                        ww_scales[:, g * OUT : (g + 1) * OUT],
+                    )
+                quantise(nc, hn_grp[:], hn_codes[:], hn_scales[:])
+                second_matmul_pass(0, hn_codes, hn_scales)
+        ha_codes = keep.tile([P, P], U32, align_bytes=64)
+        ha_scales = keep.tile([P, P], U8, align_bytes=64)
+        quantise(nc, ha_grp[:].rearrange("p n t -> p (n t)"), ha_codes[:], ha_scales[:])
+
+        second_matmul_pass(1, ha_codes, ha_scales)
+
+        pre2 = keep.tile([P, OUT], F32)
+        nc.vector.tensor_tensor(out=pre2[:], in0=h2_acc[:], in1=bw_all[:], op=ALU.add)
+        h2 = keep.tile([P, OUT], F32)
+        leaky_relu(nc, h2[:], pre2[:])
+        squares = keep.tile([P, OUT], F32)
+        sum_sq = keep.tile([P, 1], F32)
+        nc.scalar.activation(out=squares[:], in_=h2[:], func=ACT.Square, accum_out=sum_sq[:])
+        sum_sq_safe = keep.tile([P, 1], F32)
+        one_where_zero(nc, sum_sq_safe[:], sum_sq[:])
+        norm = keep.tile([P, 1], F32)
+        nc.scalar.activation(out=norm[:], in_=sum_sq_safe[:], func=ACT.Sqrt)
+        norm_rec = keep.tile([P, 1], F32)
+        nc.vector.reciprocal(out=norm_rec[:], in_=norm[:])
+        result = keep.tile([P, OUT], F32)
+        nc.vector.tensor_scalar(out=result[:], in0=h2[:], scalar1=norm_rec[:, 0:1], scalar2=None, op0=ALU.mult)
+        nc.sync.dma_start(out=out, in_=result[:])

@@ -51,6 +51,7 @@ def tile_pinsageconv_s_kernel(tc, h_node, h_ngbrs, alpha, Wq, bq, Ww, bw, out):
         work = ctx.enter_context(tc.tile_pool(name="work", bufs=4))
         held = ctx.enter_context(tc.psum_pool(name="held", bufs=1))
         banks = ctx.enter_context(tc.psum_pool(name="banks", bufs=6))
+        ctx.enter_context(tc.manual_schedule())
 
         alpha_sb = keep.tile([P, NGBR], BF16)
         nc.scalar.dma_start(out=alpha_sb[:], in_=alpha.rearrange("n k o -> n (k o)"))
@@ -113,7 +114,6 @@ def tile_pinsageconv_s_kernel(tc, h_node, h_ngbrs, alpha, Wq, bq, Ww, bw, out):
         x_scales = keep.tile([P, NGBR * P], U8, align_bytes=64)
         wq_codes = keep.tile([P, HID], U32, align_bytes=64)
         wq_scales = keep.tile([P, HID], U8, align_bytes=64)
-        copies = [nc.scalar.copy, nc.vector.tensor_copy]
         for words, grp in ((x_words, x_grp), (wq_words, wq_grp)):
             grp_words = grp[:].bitcast(F32)
             for h in range(2):
@@ -123,13 +123,19 @@ def tile_pinsageconv_s_kernel(tc, h_node, h_ngbrs, alpha, Wq, bq, Ww, bw, out):
                     ident[:],
                     [words[:, b * WORDS : (b + 1) * WORDS] for b in (2 * h, 2 * h + 1)],
                     grp_words[:, h * 4 * P : (h + 1) * 4 * P],
-                    copies[h],
+                    nc.scalar.copy,
                 )
         w_all = held.tile([P, NGBR, P], F32)
         for k in range(NGBR):
             nc.tensor.transpose(w_all[:, k, :], w_rep[:, k, :], ident[:])
         quantise(nc, x_grp[:], x_codes[:], x_scales[:])
-        quantise(nc, wq_grp[:], wq_codes[:], wq_scales[:])
+        for h in range(2):
+            quantise(
+                nc,
+                wq_grp[:, h * 2 * PACK * P : (h + 1) * 2 * PACK * P],
+                wq_codes[:, h * 2 * P : (h + 1) * 2 * P],
+                wq_scales[:, h * 2 * P : (h + 1) * 2 * P],
+            )
 
         h1_acc = []
         for t in range(PACK):
@@ -186,8 +192,8 @@ def tile_pinsageconv_s_kernel(tc, h_node, h_ngbrs, alpha, Wq, bq, Ww, bw, out):
             )
 
         ha_grp = keep.tile([P, P, PACK], BF16, align_bytes=64)
-        for pair in range(2):
-            blocks = (2 * pair, 2 * pair + 1)
+
+        def h_agg_blocks(blocks):
             h1 = {}
             weighted = {}
             for t in blocks:
@@ -206,16 +212,18 @@ def tile_pinsageconv_s_kernel(tc, h_node, h_ngbrs, alpha, Wq, bq, Ww, bw, out):
                         axis=AXIS.X,
                         op=ALU.add,
                     )
-            if pair == 0:
-                for g in range(2):
-                    quantise(
-                        nc,
-                        ww_grp[:, g * PACK * OUT : (g + 1) * PACK * OUT],
-                        ww_codes[:, g * OUT : (g + 1) * OUT],
-                        ww_scales[:, g * OUT : (g + 1) * OUT],
-                    )
-                quantise(nc, hn_grp[:], hn_codes[:], hn_scales[:])
-                second_matmul_pass(0, hn_codes, hn_scales)
+
+        h_agg_blocks((0, 1))
+        for g in range(2):
+            quantise(
+                nc,
+                ww_grp[:, g * PACK * OUT : (g + 1) * PACK * OUT],
+                ww_codes[:, g * OUT : (g + 1) * OUT],
+                ww_scales[:, g * OUT : (g + 1) * OUT],
+            )
+        quantise(nc, hn_grp[:], hn_codes[:], hn_scales[:])
+        second_matmul_pass(0, hn_codes, hn_scales)
+        h_agg_blocks((2, 3))
         ha_codes = keep.tile([P, P], U32, align_bytes=64)
         ha_scales = keep.tile([P, P], U8, align_bytes=64)
         quantise(nc, ha_grp[:].rearrange("p n t -> p (n t)"), ha_codes[:], ha_scales[:])

@@ -105,6 +105,8 @@ def tile_pinsageconv_s_kernel(tc, h_node, h_ngbrs, alpha, Wq, bq, Ww, bw, out):
         )
         bq_col = keep.tile([P, PACK], F32)
         nc.vector.tensor_copy(out=bq_col[:], in_=bq_bf[:])
+        bq_leak = keep.tile([P, PACK], F32)
+        nc.vector.tensor_scalar(out=bq_leak[:], in0=bq_bf[:], scalar1=NEG_SLOPE, scalar2=None, op0=ALU.mult)
 
         x_words = x_rows[:].bitcast(F32)
         wq_words = wq_rows[:].bitcast(F32)
@@ -136,6 +138,8 @@ def tile_pinsageconv_s_kernel(tc, h_node, h_ngbrs, alpha, Wq, bq, Ww, bw, out):
                 wq_codes[:, h * 2 * P : (h + 1) * 2 * P],
                 wq_scales[:, h * 2 * P : (h + 1) * 2 * P],
             )
+        w_sb = keep.tile([P, NGBR * P], F32)
+        nc.vector.tensor_copy(out=w_sb[:], in_=w_all[:].rearrange("p k n -> p (k n)"))
 
         h1_acc = []
         for t in range(PACK):
@@ -150,13 +154,22 @@ def tile_pinsageconv_s_kernel(tc, h_node, h_ngbrs, alpha, Wq, bq, Ww, bw, out):
                 stop=True,
             )
             h1_acc.append(acc)
-        pre = []
+        ON_GPSIMD = PACK - 1
+        weighted = []
+        h1 = []
         for t in range(PACK):
-            pre_t = work.tile([P, NGBR * P], F32, name="pre%d" % t, tag="pre")
+            leak = work.tile([P, NGBR * P], F32, name="leak%d" % t, tag="leak")
             nc.scalar.activation(
-                out=pre_t[:], in_=h1_acc[t][:], func=ACT.Identity, bias=bq_col[:, t : t + 1], scale=1.0
+                out=leak[:], in_=h1_acc[t][:], func=ACT.Identity, bias=bq_leak[:, t : t + 1], scale=NEG_SLOPE
             )
-            pre.append(pre_t)
+            h1_t = work.tile([P, NGBR * P], F32, name="h1_%d" % t, tag="h1")
+            nc.vector.scalar_tensor_tensor(
+                out=h1_t[:], in0=h1_acc[t][:], scalar=bq_col[:, t : t + 1], in1=leak[:], op0=ALU.add, op1=ALU.max
+            )
+            h1.append(h1_t)
+            weighted.append(work.tile([P, NGBR * P], F32, name="weighted%d" % t, tag="weighted"))
+        for t in range(ON_GPSIMD):
+            nc.gpsimd.tensor_tensor(out=weighted[t][:], in0=h1[t][:], in1=w_sb[:], op=ALU.mult)
 
         ww_words = ww_rows[:].bitcast(F32)
         ww_grp = keep.tile([P, 2 * PACK * OUT], BF16, align_bytes=64)
@@ -192,28 +205,18 @@ def tile_pinsageconv_s_kernel(tc, h_node, h_ngbrs, alpha, Wq, bq, Ww, bw, out):
             )
 
         ha_grp = keep.tile([P, P, PACK], BF16, align_bytes=64)
-
-        def h_agg_blocks(blocks):
-            h1 = {}
-            weighted = {}
-            for t in blocks:
-                h1[t] = work.tile([P, NGBR * P], F32, name="h1_%d" % t, tag="h1")
-                leaky_relu(nc, h1[t][:], pre[t][:])
-            for t in blocks:
-                weighted[t] = work.tile([P, NGBR * P], F32, name="weighted%d" % t, tag="weighted")
-                nc.vector.tensor_tensor(
-                    out=weighted[t][:], in0=h1[t][:], in1=w_all[:].rearrange("p k n -> p (k n)"), op=ALU.mult
+        for t in range(ON_GPSIMD, PACK):
+            nc.vector.tensor_tensor(
+                out=weighted[t][:], in0=h1[t][:], in1=w_all[:].rearrange("p k n -> p (k n)"), op=ALU.mult
+            )
+        for t in range(PACK):
+            with nc.allow_low_precision(reason="the sum is float32; h_agg is rounded once to bfloat16"):
+                nc.vector.tensor_reduce(
+                    out=ha_grp[:, :, t],
+                    in_=weighted[t][:].rearrange("p (k n) -> p n k", k=NGBR),
+                    axis=AXIS.X,
+                    op=ALU.add,
                 )
-            for t in blocks:
-                with nc.allow_low_precision(reason="the sum is float32; h_agg is rounded once to bfloat16"):
-                    nc.vector.tensor_reduce(
-                        out=ha_grp[:, :, t],
-                        in_=weighted[t][:].rearrange("p (k n) -> p n k", k=NGBR),
-                        axis=AXIS.X,
-                        op=ALU.add,
-                    )
-
-        h_agg_blocks((0, 1))
         for g in range(2):
             quantise(
                 nc,
@@ -223,7 +226,6 @@ def tile_pinsageconv_s_kernel(tc, h_node, h_ngbrs, alpha, Wq, bq, Ww, bw, out):
             )
         quantise(nc, hn_grp[:], hn_codes[:], hn_scales[:])
         second_matmul_pass(0, hn_codes, hn_scales)
-        h_agg_blocks((2, 3))
         ha_codes = keep.tile([P, P], U32, align_bytes=64)
         ha_scales = keep.tile([P, P], U8, align_bytes=64)
         quantise(nc, ha_grp[:].rearrange("p n t -> p (n t)"), ha_codes[:], ha_scales[:])

@@ -19,6 +19,7 @@ K_PASS = P * PACK
 WORDS = K_PASS // 2
 IN, HID, OUT = 512, 512, 512
 NEG_SLOPE = 0.01
+SMALLEST_NORMAL = 2.0**-126
 
 FLOPS = 2 * (P * NGBR) * IN * HID + 2 * P * (IN + HID) * OUT
 
@@ -54,21 +55,24 @@ def tile_pinsageconv_s_kernel(tc, h_node, h_ngbrs, alpha, Wq, bq, Ww, bw, out):
         ctx.enter_context(tc.manual_schedule())
 
         alpha_sb = keep.tile([P, NGBR], BF16)
-        nc.scalar.dma_start(out=alpha_sb[:], in_=alpha.rearrange("n k o -> n (k o)"))
+        nc.sync.dma_start(out=alpha_sb[:], in_=alpha.rearrange("n k o -> n (k o)"))
         bq_bf = keep.tile([P, PACK], BF16)
         nc.scalar.dma_start(
             out=bq_bf[:].rearrange("p (u e) -> p u e", e=2), in_=bq.rearrange("(u p e) -> p u e", u=2, e=2)
         )
 
-        x_rows = keep.tile([P, NGBR * IN], BF16)
-        x_dram = h_ngbrs.rearrange("n k i -> n (k i)")
+        x_rows = keep.tile([P, 4 * IN], BF16)
+        x_dram = h_ngbrs.rearrange("n k i -> (n k) i")
         wq_rows = keep.tile([P, PACK * IN], BF16)
         ww_rows = keep.tile([P, 4 * (IN + HID)], BF16)
         hn_rows = keep.tile([P, IN], BF16)
         bw_all = keep.tile([P, OUT], BF16)
         half = 2 * IN
         for h in range(2):
-            nc.sync.dma_start(out=x_rows[:, h * half : (h + 1) * half], in_=x_dram[:, h * half : (h + 1) * half])
+            nc.sync.dma_start(
+                out=x_rows[:, h * half : (h + 1) * half].rearrange("p (b i) -> p b i", b=2),
+                in_=x_dram[h * 2 * P : (h + 1) * 2 * P, :].rearrange("(b p) i -> p b i", p=P),
+            )
         for u in range(2):
             nc.sync.dma_start(
                 out=wq_rows[:, u * half : (u + 1) * half],
@@ -103,10 +107,6 @@ def tile_pinsageconv_s_kernel(tc, h_node, h_ngbrs, alpha, Wq, bq, Ww, bw, out):
             scalar2=None,
             op0=ALU.mult,
         )
-        bq_col = keep.tile([P, PACK], F32)
-        nc.vector.tensor_copy(out=bq_col[:], in_=bq_bf[:])
-        bq_leak = keep.tile([P, PACK], F32)
-        nc.vector.tensor_scalar(out=bq_leak[:], in0=bq_bf[:], scalar1=NEG_SLOPE, scalar2=None, op0=ALU.mult)
 
         x_words = x_rows[:].bitcast(F32)
         wq_words = wq_rows[:].bitcast(F32)
@@ -138,8 +138,14 @@ def tile_pinsageconv_s_kernel(tc, h_node, h_ngbrs, alpha, Wq, bq, Ww, bw, out):
                 wq_codes[:, h * 2 * P : (h + 1) * 2 * P],
                 wq_scales[:, h * 2 * P : (h + 1) * 2 * P],
             )
-        w_sb = keep.tile([P, NGBR * P], F32)
-        nc.vector.tensor_copy(out=w_sb[:], in_=w_all[:].rearrange("p k n -> p (k n)"))
+        w_sb = keep.tile([P, P * NGBR], F32)
+        nc.vector.tensor_copy(
+            out=w_sb[:].rearrange("p (n k) -> p n k", k=NGBR), in_=w_all[:].rearrange("p k n -> p n k")
+        )
+        bq_col = keep.tile([P, PACK], F32)
+        nc.vector.tensor_copy(out=bq_col[:], in_=bq_bf[:])
+        bq_leak = keep.tile([P, PACK], F32)
+        nc.vector.tensor_scalar(out=bq_leak[:], in0=bq_bf[:], scalar1=NEG_SLOPE, scalar2=None, op0=ALU.mult)
 
         h1_acc = []
         for t in range(PACK):
@@ -154,22 +160,23 @@ def tile_pinsageconv_s_kernel(tc, h_node, h_ngbrs, alpha, Wq, bq, Ww, bw, out):
                 stop=True,
             )
             h1_acc.append(acc)
-        ON_GPSIMD = PACK - 1
-        weighted = []
-        h1 = []
+        h1 = [work.tile([P, 2, NGBR * P], F32, name="h1_pair%d" % j, tag="h1") for j in range(2)]
+        weighted = [work.tile([P, 2, NGBR * P], F32, name="weighted_pair%d" % j, tag="weighted") for j in range(2)]
         for t in range(PACK):
             leak = work.tile([P, NGBR * P], F32, name="leak%d" % t, tag="leak")
             nc.scalar.activation(
                 out=leak[:], in_=h1_acc[t][:], func=ACT.Identity, bias=bq_leak[:, t : t + 1], scale=NEG_SLOPE
             )
-            h1_t = work.tile([P, NGBR * P], F32, name="h1_%d" % t, tag="h1")
             nc.vector.scalar_tensor_tensor(
-                out=h1_t[:], in0=h1_acc[t][:], scalar=bq_col[:, t : t + 1], in1=leak[:], op0=ALU.add, op1=ALU.max
+                out=h1[t // 2][:, t % 2, :],
+                in0=h1_acc[t][:],
+                scalar=bq_col[:, t : t + 1],
+                in1=leak[:],
+                op0=ALU.add,
+                op1=ALU.max,
             )
-            h1.append(h1_t)
-            weighted.append(work.tile([P, NGBR * P], F32, name="weighted%d" % t, tag="weighted"))
-        for t in range(ON_GPSIMD):
-            nc.gpsimd.tensor_tensor(out=weighted[t][:], in0=h1[t][:], in1=w_sb[:], op=ALU.mult)
+        for i in range(2):
+            nc.gpsimd.tensor_tensor(out=weighted[0][:, i, :], in0=h1[0][:, i, :], in1=w_sb[:], op=ALU.mult)
 
         ww_words = ww_rows[:].bitcast(F32)
         ww_grp = keep.tile([P, 2 * PACK * OUT], BF16, align_bytes=64)
@@ -205,15 +212,17 @@ def tile_pinsageconv_s_kernel(tc, h_node, h_ngbrs, alpha, Wq, bq, Ww, bw, out):
             )
 
         ha_grp = keep.tile([P, P, PACK], BF16, align_bytes=64)
-        for t in range(ON_GPSIMD, PACK):
-            nc.vector.tensor_tensor(
-                out=weighted[t][:], in0=h1[t][:], in1=w_all[:].rearrange("p k n -> p (k n)"), op=ALU.mult
-            )
-        for t in range(PACK):
+        nc.vector.tensor_tensor(
+            out=weighted[1][:].rearrange("p t (n k) -> p t n k", k=NGBR),
+            in0=h1[1][:].rearrange("p t (n k) -> p t n k", k=NGBR),
+            in1=w_all[:].rearrange("p k n -> p n k").unsqueeze(1).to_broadcast([P, 2, P, NGBR]),
+            op=ALU.mult,
+        )
+        for j in range(2):
             with nc.allow_low_precision(reason="the sum is float32; h_agg is rounded once to bfloat16"):
                 nc.vector.tensor_reduce(
-                    out=ha_grp[:, :, t],
-                    in_=weighted[t][:].rearrange("p (k n) -> p n k", k=NGBR),
+                    out=ha_grp[:, :, 2 * j : 2 * j + 2].rearrange("p n t -> p t n"),
+                    in_=weighted[j][:].rearrange("p t (n k) -> p t n k", k=NGBR),
                     axis=AXIS.X,
                     op=ALU.add,
                 )
@@ -239,12 +248,12 @@ def tile_pinsageconv_s_kernel(tc, h_node, h_ngbrs, alpha, Wq, bq, Ww, bw, out):
         squares = keep.tile([P, OUT], F32)
         sum_sq = keep.tile([P, 1], F32)
         nc.scalar.activation(out=squares[:], in_=h2[:], func=ACT.Square, accum_out=sum_sq[:])
-        sum_sq_safe = keep.tile([P, 1], F32)
-        one_where_zero(nc, sum_sq_safe[:], sum_sq[:])
         norm = keep.tile([P, 1], F32)
-        nc.scalar.activation(out=norm[:], in_=sum_sq_safe[:], func=ACT.Sqrt)
+        nc.scalar.activation(out=norm[:], in_=sum_sq[:], func=ACT.Sqrt)
+        norm_safe = keep.tile([P, 1], F32)
+        nc.vector.tensor_scalar(out=norm_safe[:], in0=norm[:], scalar1=SMALLEST_NORMAL, scalar2=None, op0=ALU.max)
         norm_rec = keep.tile([P, 1], F32)
-        nc.vector.reciprocal(out=norm_rec[:], in_=norm[:])
+        nc.vector.reciprocal(out=norm_rec[:], in_=norm_safe[:])
         result = keep.tile([P, OUT], F32)
         nc.vector.tensor_scalar(out=result[:], in0=h2[:], scalar1=norm_rec[:, 0:1], scalar2=None, op0=ALU.mult)
         nc.sync.dma_start(out=out, in_=result[:])

from contextlib import ExitStack

import concourse.mybir as mybir
from concourse.masks import make_identity

F32 = mybir.dt.float32
BF16 = mybir.dt.bfloat16
U32 = mybir.dt.uint32
U8 = mybir.dt.uint8
FP8X4 = mybir.dt.float8_e4m3fn_x4
ALU = mybir.AluOpType
ACT = mybir.ActivationFunctionType
AXIS = mybir.AxisListType

P = 128
NGBR = 4
PACK = 4
K_PASS = P * PACK
WORDS = K_PASS // 2
IN, HID, OUT = 512, 512, 512
NEG_SLOPE = 0.01
SMALLEST_NORMAL = 2.0**-126

FLOPS = 2 * (P * NGBR) * IN * HID + 2 * P * (IN + HID) * OUT


def turn_blocks(nc, banks, ident, blocks, grouped, copy):
    rows = P * len(blocks)
    bank = banks.tile([P, 2, rows], F32, tag="bank")
    for b, block in enumerate(blocks):
        for u in range(2):
            nc.tensor.transpose(bank[:, u, b * P : (b + 1) * P], block[:, u * P : (u + 1) * P], ident)
    copy(out=grouped.rearrange("p (r u) -> p r u", u=2), in_=bank[:].rearrange("p u r -> p r u"))


def quantise(nc, grouped, codes, scales):
    nc.vector.quantize_mx(out=codes.bitcast(FP8X4), scales=scales, in_=grouped)


def leaky_relu(nc, out, in_):
    nc.vector.scalar_tensor_tensor(out=out, in0=in_, scalar=NEG_SLOPE, in1=in_, op0=ALU.mult, op1=ALU.max)


def one_where_zero(nc, out, in_):
    nc.vector.scalar_tensor_tensor(out=out, in0=in_, scalar=0.0, in1=in_, op0=ALU.is_equal, op1=ALU.add)


def tile_pinsageconv_s_kernel(tc, h_node, h_ngbrs, alpha, Wq, bq, Ww, bw, out):
    nc = tc.nc
    with ExitStack() as ctx:
        keep = ctx.enter_context(tc.tile_pool(name="keep", bufs=1))
        work = ctx.enter_context(tc.tile_pool(name="work", bufs=4))
        held = ctx.enter_context(tc.psum_pool(name="held", bufs=1))
        banks = ctx.enter_context(tc.psum_pool(name="banks", bufs=6))
        ctx.enter_context(tc.manual_schedule())

        alpha_sb = keep.tile([P, NGBR], BF16)
        nc.sync.dma_start(out=alpha_sb[:], in_=alpha.rearrange("n k o -> n (k o)"))
        bq_bf = keep.tile([P, PACK], BF16)
        nc.scalar.dma_start(
            out=bq_bf[:].rearrange("p (u e) -> p u e", e=2), in_=bq.rearrange("(u p e) -> p u e", u=2, e=2)
        )

        x_rows = keep.tile([P, 4 * IN], BF16)
        x_dram = h_ngbrs.rearrange("n k i -> (n k) i")
        wq_rows = keep.tile([P, PACK * IN], BF16)
        ww_rows = keep.tile([P, 4 * (IN + HID)], BF16)
        hn_rows = keep.tile([P, IN], BF16)
        bw_all = keep.tile([P, OUT], BF16)
        half = 2 * IN
        for h in range(2):
            nc.sync.dma_start(
                out=x_rows[:, h * half : (h + 1) * half].rearrange("p (b i) -> p b i", b=2),
                in_=x_dram[h * 2 * P : (h + 1) * 2 * P, :].rearrange("(b p) i -> p b i", p=P),
            )
        for u in range(2):
            nc.sync.dma_start(
                out=wq_rows[:, u * half : (u + 1) * half],
                in_=Wq[u * 2 * P : (u + 1) * 2 * P, :].rearrange("(p e) i -> p (e i)", e=2),
            )
        for h in range(2):
            nc.sync.dma_start(
                out=ww_rows[:, h * 2 * (IN + HID) : (h + 1) * 2 * (IN + HID)].rearrange("p (r j) -> p r j", r=2),
                in_=Ww[h * 2 * P : (h + 1) * 2 * P, :].rearrange("(r p) j -> p r j", p=P),
            )
        nc.sync.dma_start(out=hn_rows[:], in_=h_node)
        nc.sync.dma_start(out=bw_all[:], in_=bw.partition_broadcast(P))

        ident = keep.tile([P, P], F32)
        make_identity(nc, ident[:])
        one = keep.tile([P, 1], F32)
        nc.vector.memset(one[:], 1.0)
        root_of_one = keep.tile([P, 1], F32)
        nc.scalar.activation(out=root_of_one[:], in_=one[:], func=ACT.Sqrt)

        alpha_sum = keep.tile([P, 1], F32)
        nc.vector.tensor_reduce(out=alpha_sum[:], in_=alpha_sb[:], axis=AXIS.X, op=ALU.add)
        alpha_den = keep.tile([P, 1], F32)
        one_where_zero(nc, alpha_den[:], alpha_sum[:])
        alpha_rec = keep.tile([P, 1], F32)
        nc.vector.reciprocal(out=alpha_rec[:], in_=alpha_den[:])
        w_rep = keep.tile([P, NGBR, P], F32)
        nc.vector.tensor_scalar(
            out=w_rep[:],
            in0=alpha_sb[:].unsqueeze(2).to_broadcast([P, NGBR, P]),
            scalar1=alpha_rec[:, 0:1],
            scalar2=None,
            op0=ALU.mult,
        )

        x_words = x_rows[:].bitcast(F32)
        wq_words = wq_rows[:].bitcast(F32)
        x_grp = keep.tile([P, PACK * NGBR * P], BF16, align_bytes=64)
        wq_grp = keep.tile([P, PACK * HID], BF16, align_bytes=64)
        x_codes = keep.tile([P, NGBR * P], U32, align_bytes=64)
        x_scales = keep.tile([P, NGBR * P], U8, align_bytes=64)
        wq_codes = keep.tile([P, HID], U32, align_bytes=64)
        wq_scales = keep.tile([P, HID], U8, align_bytes=64)
        for words, grp in ((x_words, x_grp), (wq_words, wq_grp)):
            grp_words = grp[:].bitcast(F32)
            for h in range(2):
                turn_blocks(
                    nc,
                    banks,
                    ident[:],
                    [words[:, b * WORDS : (b + 1) * WORDS] for b in (2 * h, 2 * h + 1)],
                    grp_words[:, h * 4 * P : (h + 1) * 4 * P],
                    nc.scalar.copy,
                )
        w_all = held.tile([P, NGBR, P], F32)
        for k in range(NGBR):
            nc.tensor.transpose(w_all[:, k, :], w_rep[:, k, :], ident[:])
        quantise(nc, x_grp[:], x_codes[:], x_scales[:])
        for h in range(2):
            quantise(
                nc,
                wq_grp[:, h * 2 * PACK * P : (h + 1) * 2 * PACK * P],
                wq_codes[:, h * 2 * P : (h + 1) * 2 * P],
                wq_scales[:, h * 2 * P : (h + 1) * 2 * P],
            )
        w_sb = keep.tile([P, P * NGBR], F32)
        nc.vector.tensor_copy(
            out=w_sb[:].rearrange("p (n k) -> p n k", k=NGBR), in_=w_all[:].rearrange("p k n -> p n k")
        )
        bq_col = keep.tile([P, PACK], F32)
        nc.vector.tensor_copy(out=bq_col[:], in_=bq_bf[:])
        bq_leak = keep.tile([P, PACK], F32)
        nc.vector.tensor_scalar(out=bq_leak[:], in0=bq_bf[:], scalar1=NEG_SLOPE, scalar2=None, op0=ALU.mult)

        h1_acc = []
        for t in range(PACK):
            acc = banks.tile([P, NGBR * P], F32, tag="bank", name="h1_acc%d" % t)
            nc.tensor.matmul_mx(
                out=acc[:],
                lhsT=wq_codes[:, t * P : (t + 1) * P].bitcast(FP8X4),
                lhsT_scale=wq_scales[:, t * P : (t + 1) * P],
                rhs=x_codes[:].bitcast(FP8X4),
                rhs_scale=x_scales[:],
                start=True,
                stop=True,
            )
            h1_acc.append(acc)
        h1 = [work.tile([P, 2, NGBR * P], F32, name="h1_pair%d" % j, tag="h1") for j in range(2)]
        weighted = [work.tile([P, 2, NGBR * P], F32, name="weighted_pair%d" % j, tag="weighted") for j in range(2)]
        for t in range(PACK):
            leak = work.tile([P, NGBR * P], F32, name="leak%d" % t, tag="leak")
            nc.scalar.activation(
                out=leak[:], in_=h1_acc[t][:], func=ACT.Identity, bias=bq_leak[:, t : t + 1], scale=NEG_SLOPE
            )
            nc.vector.scalar_tensor_tensor(
                out=h1[t // 2][:, t % 2, :],
                in0=h1_acc[t][:],
                scalar=bq_col[:, t : t + 1],
                in1=leak[:],
                op0=ALU.add,
                op1=ALU.max,
            )
        for i in range(2):
            nc.gpsimd.tensor_tensor(out=weighted[0][:, i, :], in0=h1[0][:, i, :], in1=w_sb[:], op=ALU.mult)

        ww_words = ww_rows[:].bitcast(F32)
        ww_grp = keep.tile([P, 2 * PACK * OUT], BF16, align_bytes=64)
        ww_grp_words = ww_grp[:].bitcast(F32)
        ww_codes = keep.tile([P, 2 * OUT], U32, align_bytes=64)
        ww_scales = keep.tile([P, 2 * OUT], U8, align_bytes=64)
        hn_grp = keep.tile([P, PACK * P], BF16, align_bytes=64)
        hn_codes = keep.tile([P, P], U32, align_bytes=64)
        hn_scales = keep.tile([P, P], U8, align_bytes=64)
        for g in range(2):
            for h in range(2):
                turn_blocks(
                    nc,
                    banks,
                    ident[:],
                    [ww_words[:, (2 * r + g) * WORDS : (2 * r + g + 1) * WORDS] for r in (2 * h, 2 * h + 1)],
                    ww_grp_words[:, (2 * g + h) * 4 * P : (2 * g + h + 1) * 4 * P],
                    nc.scalar.copy,
                )
        turn_blocks(nc, banks, ident[:], [hn_rows[:].bitcast(F32)], hn_grp[:].bitcast(F32), nc.scalar.copy)

        h2_acc = held.tile([P, OUT], F32)

        def second_matmul_pass(g, codes, scales):
            nc.tensor.matmul_mx(
                out=h2_acc[:],
                lhsT=codes[:].bitcast(FP8X4),
                lhsT_scale=scales[:],
                rhs=ww_codes[:, g * OUT : (g + 1) * OUT].bitcast(FP8X4),
                rhs_scale=ww_scales[:, g * OUT : (g + 1) * OUT],
                start=(g == 0),
                stop=(g == 1),
            )

        ha_grp = keep.tile([P, P, PACK], BF16, align_bytes=64)
        nc.vector.tensor_tensor(
            out=weighted[1][:].rearrange("p t (n k) -> p t n k", k=NGBR),
            in0=h1[1][:].rearrange("p t (n k) -> p t n k", k=NGBR),
            in1=w_all[:].rearrange("p k n -> p n k").unsqueeze(1).to_broadcast([P, 2, P, NGBR]),
            op=ALU.mult,
        )
        for j in range(2):
            with nc.allow_low_precision(reason="the sum is float32; h_agg is rounded once to bfloat16"):
                nc.vector.tensor_reduce(
                    out=ha_grp[:, :, 2 * j : 2 * j + 2].rearrange("p n t -> p t n"),
                    in_=weighted[j][:].rearrange("p t (n k) -> p t n k", k=NGBR),
                    axis=AXIS.X,
                    op=ALU.add,
                )
        for g in range(2):
            quantise(
                nc,
                ww_grp[:, g * PACK * OUT : (g + 1) * PACK * OUT],
                ww_codes[:, g * OUT : (g + 1) * OUT],
                ww_scales[:, g * OUT : (g + 1) * OUT],
            )
        quantise(nc, hn_grp[:], hn_codes[:], hn_scales[:])
        second_matmul_pass(0, hn_codes, hn_scales)
        ha_codes = keep.tile([P, P], U32, align_bytes=64)
        ha_scales = keep.tile([P, P], U8, align_bytes=64)
        quantise(nc, ha_grp[:].rearrange("p n t -> p (n t)"), ha_codes[:], ha_scales[:])

        second_matmul_pass(1, ha_codes, ha_scales)

        pre2 = keep.tile([P, OUT], F32)
        nc.vector.tensor_tensor(out=pre2[:], in0=h2_acc[:], in1=bw_all[:], op=ALU.add)
        h2 = keep.tile([P, OUT], F32)
        leaky_relu(nc, h2[:], pre2[:])
        squares = keep.tile([P, OUT], F32)
        sum_sq = keep.tile([P, 1], F32)
        nc.scalar.activation(out=squares[:], in_=h2[:], func=ACT.Square, accum_out=sum_sq[:])
        norm = keep.tile([P, 1], F32)
        nc.scalar.activation(out=norm[:], in_=sum_sq[:], func=ACT.Sqrt)
        norm_safe = keep.tile([P, 1], F32)
        nc.vector.tensor_scalar(out=norm_safe[:], in0=norm[:], scalar1=SMALLEST_NORMAL, scalar2=None, op0=ALU.max)
        norm_rec = keep.tile([P, 1], F32)
        nc.vector.reciprocal(out=norm_rec[:], in_=norm_safe[:])
        result = keep.tile([P, OUT], F32)
        nc.vector.tensor_scalar(out=result[:], in0=h2[:], scalar1=norm_rec[:, 0:1], scalar2=None, op0=ALU.mult)
        nc.sync.dma_start(out=out, in_=result[:])
